import numpy as np
import ml_dtypes


def mxq(x, axis, fmt="e4m3"):
    dtype, down = {"e4m3": (ml_dtypes.float8_e4m3fn, 7), "e5m2": (ml_dtypes.float8_e5m2, 14)}[fmt]
    v = np.moveaxis(np.asarray(x, np.float32).astype(ml_dtypes.bfloat16).astype(np.float64), axis, -1)
    blocks = v.reshape(v.shape[:-1] + (-1, 32))
    amax = np.abs(blocks).max(-1, keepdims=True)
    byte = np.maximum(np.where(amax > 0, np.frexp(amax)[1] - 1 + 127, 0) - down, 1)
    scale = np.exp2(byte - 127.0)
    codes = (blocks / scale).astype(np.float32).astype(dtype).astype(np.float64)
    return np.moveaxis((codes * scale).reshape(v.shape), -1, axis)


WIDE = False


def mx_kscale(k):
    if not WIDE:
        return np.ones(k)
    levels = np.array([18, -18])
    if k % 512:
        return np.exp2(np.random.permutation(np.resize(levels, k // 32))).repeat(32)
    a = np.empty((k // 512, 16))
    for p in range(k // 512):
        a[p, :8] = np.random.permutation(np.resize(levels, 8))
        for g in range(8):
            far = levels[np.abs(levels - a[p, g]) >= 10]
            a[p, g + 8] = far[np.random.randint(len(far))]
    return np.exp2(a.ravel()).repeat(32)


BF16 = ml_dtypes.bfloat16


def bf(x):
    return np.asarray(x, np.float32).astype(BF16)


def f64(x):
    return np.asarray(x).astype(np.float64)


B, IN, HID, CENT = 1024, 128, 512, 2048


def setup_inputs():
    s = mx_kscale(B)[:, None]
    u = mx_kscale(CENT)
    v = mx_kscale(HID)
    sigmas = bf(1.0 + 0.1 * np.random.standard_normal(HID))
    c0 = bf(np.random.standard_normal((HID, IN)) / np.sqrt(IN))
    x0 = bf(np.random.standard_normal((B, IN)) / np.sqrt(IN))
    w1_0 = bf(np.random.standard_normal((CENT, HID)) * 6.0 / np.sqrt(HID))
    b1 = bf(0.2 * np.random.standard_normal(CENT))
    g = bf(np.random.standard_normal((B, CENT)) * np.exp2(np.random.randint(-6, 1, (B, 1))) / s * u)
    xf, cf, sf = f64(x0), f64(c0), f64(sigmas)
    d2 = np.maximum((xf * xf).sum(1)[:, None] + (cf * cf).sum(1)[None, :] - 2.0 * (xf @ cf.T), 0.0)
    z2 = np.exp(-d2 * (sf * sf)[None, :]) @ f64(w1_0).T + f64(b1)
    return {"x": bf(f64(x0) * s), "centres": bf(f64(c0) / v[:, None]), "sigmas": sigmas,
            "w1": bf(f64(w1_0) * v[None, :] / u[:, None]), "b1": b1,
            "d2": np.asarray(d2, np.float32), "z2": np.asarray(z2, np.float32), "grad_out": g}


def reference(x, centres, sigmas, w1, b1, d2, z2, grad_out):
    xf, cf, sf, df = f64(x), f64(centres), f64(sigmas), f64(d2)
    s2 = (sf * sf)[None, :]
    dz2 = f64(grad_out) * (f64(z2) > 0.0)
    dphi = mxq(dz2, 1, "e5m2") @ mxq(f64(w1), 1 - 1, "e4m3")
    dz1 = 2.0 * dphi * s2 * np.exp(-df * s2) * (df > 0.0)
    dx = (mxq(dz1, 1, "e5m2") @ mxq(cf, 0, "e4m3")) - xf * dz1.sum(1)[:, None]
    dc = (mxq(dz1, 0, "e5m2").T @ mxq(xf, 0, "e4m3")) - cf * dz1.sum(0)[:, None]
    return dx, dc

@@ -1,0 +1,489 @@
+from contextlib import ExitStack
+
+import concourse.mybir as mybir
+from concourse.masks import make_identity
+
+B, IN, HID, CENT = 1024, 128, 512, 2048
+FLOPS = 2 * B * CENT * HID + 2 * 2 * B * HID * IN
+BYTES = (B * CENT * 6 + B * HID * 4 + CENT * HID * 2 + B * IN * 2 + HID * IN * 2
+         + HID * 2 + B * IN * 4 + HID * IN * 4)
+
+F32 = mybir.dt.float32
+BF16 = mybir.dt.bfloat16
+U32 = mybir.dt.uint32
+U8 = mybir.dt.uint8
+E4 = mybir.dt.float8_e4m3fn_x4
+E5 = mybir.dt.float8_e5m2_x4
+ALU = mybir.AluOpType
+ACT = mybir.ActivationFunctionType
+AX = mybir.AxisListType
+P = 128
+
+UNITS = [
+    (0, 0, 1, 0, 1024), (0, 1, 1, 0, 1024), (0, 2, 2, 0, 1024),
+    (0, 0, 2, 1024, 1024), (0, 2, 2, 1024, 1024),
+    (1, 0, 2, 0, 1024), (1, 2, 2, 0, 1024),
+    (1, 0, 2, 1024, 1024), (1, 2, 2, 1024, 1024),
+]
+
+
+def tile_networkprc_pa_v_kernel(tc, x, centres, sigmas, w1, b1, d2, z2, grad_out, out_0, out_1):
+    nc = tc.nc
+    with ExitStack() as ctx:
+        keep = ctx.enter_context(tc.tile_pool(name="keep", bufs=1))
+        ypool = ctx.enter_context(tc.tile_pool(name="ypool", bufs=3))
+        gpool = ctx.enter_context(tc.tile_pool(name="gpool", bufs=2))
+        cpool = ctx.enter_context(tc.tile_pool(name="cpool", bufs=4))
+        psum = ctx.enter_context(tc.psum_pool(name="psum", bufs=1))
+        ctx.enter_context(tc.manual_schedule())
+
+        def bank(i):
+            b = psum.tile([P, 512], F32, name="bank%d" % i)
+            return b
+
+        sg = keep.tile([P, 4], BF16, name="sg")
+        craw = keep.tile([P, 4, IN], BF16, name="craw")
+        xraw = keep.tile([P, 2, 4, IN], BF16, name="xraw")
+        wraw = [keep.tile([P, 4, HID], BF16, name="wraw%d" % g) for g in range(4)]
+        draw = [keep.tile([P, 4, HID], F32, name="draw%d" % h) for h in range(2)]
+        zt = [keep.tile([P, u[2] * u[4]], F32, name="z%d" % k) for k, u in enumerate(UNITS[:7])]
+        gt = [keep.tile([P, u[2] * u[4]], BF16, name="g%d" % k) for k, u in enumerate(UNITS[:7])]
+        zt += zt[2:4]
+        gt += gt[2:4]
+
+        def load_w(g):
+            nc.sync.dma_start(out=wraw[g][:], in_=w1[512 * g:512 * g + 512, :].rearrange("(p j) c -> p j c", j=4))
+
+        def load_d(h):
+            nc.sync.dma_start(out=draw[h][:], in_=d2[512 * h:512 * h + 512, :].rearrange("(p t) c -> p t c", t=4))
+
+        def load_u(k):
+            (h, t0, nt, f0, nf) = UNITS[k]
+            for dst, src in ((zt[k], z2), (gt[k], grad_out)):
+                v = src[512 * h:512 * h + 512, f0:f0 + nf].rearrange("(p t) f -> p t f", t=4)[:, t0:t0 + nt, :]
+                nc.sync.dma_start(out=dst[:].rearrange("p (t f) -> p t f", t=nt), in_=v)
+
+        def load_s():
+            nc.sync.dma_start(out=sg[:], in_=sigmas.rearrange("(p s) -> p s", s=4))
+
+        def load_c():
+            nc.sync.dma_start(out=craw[:], in_=centres.rearrange("(p j) k -> p j k", j=4))
+
+        def load_x():
+            nc.sync.dma_start(out=xraw[:], in_=x.rearrange("(h p j) k -> p h j k", h=2, j=4))
+
+        one = keep.tile([P, 1], F32, name="one")
+        nc.gpsimd.memset(one[:], 1.0)
+        ident = keep.tile([P, P], F32, name="ident")
+        make_identity(nc, ident[:])
+        warm = keep.tile([P, 1], F32, name="warm")
+        nc.scalar.activation(out=warm[:], in_=one[:], func=ACT.Exp)
+        rcodes = keep.tile([P, 768], U32, name="rcodes", align_bytes=64)
+        rscales = keep.tile([P, 768], U8, name="rscales", align_bytes=64)
+        nc.gpsimd.memset(rcodes[:, 384:768], 0)
+        nc.gpsimd.memset(rscales[:, 384:768], 0)
+        s2 = keep.tile([P, 4], F32, name="s2")
+        negs2 = keep.tile([P, 4], F32, name="negs2")
+        twos2 = keep.tile([P, 4], F32, name="twos2")
+
+        xneg = keep.tile([P, 2, 4, IN], BF16, name="xneg")
+        cneg = keep.tile([P, 4, IN], BF16, name="cneg")
+
+        def neg():
+            nc.gpsimd.tensor_scalar(out=xneg[:], in0=xraw[:], scalar1=-1.0, scalar2=0.0, op0=ALU.mult, op1=ALU.add)
+            nc.gpsimd.tensor_scalar(out=cneg[:], in0=craw[:], scalar1=-1.0, scalar2=0.0, op0=ALU.mult, op1=ALU.add)
+
+        def sigma():
+            nc.vector.tensor_tensor(out=s2[:], in0=sg[:], in1=sg[:], op=ALU.mult)
+            nc.vector.tensor_scalar(out=negs2[:], in0=s2[:], scalar1=-1.0, scalar2=None, op0=ALU.mult)
+            nc.vector.tensor_scalar(out=twos2[:], in0=s2[:], scalar1=2.0, scalar2=None, op0=ALU.mult)
+
+        rgrp = keep.tile([P, 384, 4], BF16, name="rgrp", align_bytes=64)
+        rflat = rgrp[:].rearrange("p k j -> p (k j)")
+
+        def copy(eng, out, in_):
+            if eng == "v":
+                nc.vector.tensor_copy(out=out, in_=in_)
+            else:
+                nc.scalar.copy(out=out, in_=in_)
+
+        def cc(eng):
+            copy(eng, rgrp[:, 128:256, :], craw[:].rearrange("p j k -> p k j"))
+
+        def xc(h, eng):
+            copy(eng, rgrp[:, 256 * h:256 * h + 128, :], xraw[:, h].rearrange("p j k -> p k j"))
+
+        def rq(w0, n):
+            nc.vector.quantize_mx(out=rcodes[:, w0:w0 + n].bitcast(E4), scales=rscales[:, w0:w0 + n], in_=rflat[:, 4 * w0:4 * (w0 + n)])
+
+        wcodes = [keep.tile([P, HID], U32, name="wcodes%d" % g, align_bytes=64) for g in range(4)]
+        wscales = [keep.tile([P, HID], U8, name="wscales%d" % g, align_bytes=64) for g in range(4)]
+        wgrp = {}
+
+        def wc(g, eng):
+            wg = gpool.tile([P, HID * 4], BF16, name="wg", align_bytes=64)
+            copy(eng, wg[:].rearrange("p (s m j) -> p s m j", s=4, j=4), wraw[g][:].rearrange("p j (m s) -> p s m j", s=4))
+            wgrp[g] = wg
+
+        def wq(g):
+            nc.vector.quantize_mx(out=wcodes[g][:].bitcast(E4), scales=wscales[g][:], in_=wgrp[g][:])
+
+        ed = [keep.tile([P, 4, 512], F32, name="ed%d" % h) for h in range(2)]
+        dT = {}
+
+        big = [keep.tile([P, 4, HID], F32, name="big%d" % h) for h in range(2)]
+
+        def db(h):
+            nc.vector.tensor_scalar(out=big[h][:], in0=draw[h][:], scalar1=0.0, scalar2=3.0e38, op0=ALU.is_le, op1=ALU.mult)
+
+        def dt(h, s, b):
+            bk = bank(b)
+            for t in range(4):
+                cols = bk[:, 128 * t:128 * t + 128]
+                nc.tensor.matmul(cols, lhsT=draw[h][:, t, s:512:4], rhs=ident[:], start=True, stop=False, is_transpose=True)
+                nc.tensor.matmul(cols, lhsT=big[h][:, t, s:512:4], rhs=ident[:], start=False, stop=True, is_transpose=True)
+            dT[(h, s)] = bk
+
+        def dx(h, s):
+            nc.scalar.activation(out=ed[h][:, s, :], in_=dT[(h, s)][:], func=ACT.Exp, scale=negs2[:, s:s + 1])
+
+        yt = {}
+        grp = {}
+
+        def m(k):
+            (h, t0, nt, f0, nf) = UNITS[k]
+            y = ypool.tile([P, nt * nf], BF16, name="y")
+            half = nt * nf // 2
+            zv = zt[k][:].rearrange("p (q u e) -> p u q e", u=2, e=2)
+            gv = gt[k][:].rearrange("p (q u e) -> p u q e", u=2, e=2)
+            for u in range(2):
+                nc.vector.scalar_tensor_tensor(
+                    out=y[:, u * half:(u + 1) * half].rearrange("p (q e) -> p q e", e=2),
+                    in0=zv[:, u], scalar=0.0, in1=gv[:, u], op0=ALU.is_gt, op1=ALU.mult)
+            yt[k] = y
+
+        zb = {}
+
+        def ut(k, i, b):
+            (h, t0, nt, f0, nf) = UNITS[k]
+            words = yt[k][:].bitcast(F32)
+            n = 128 * nt
+            bk = bank(b)
+            for g in range(2 // nt):
+                for u in range(2):
+                    for t in range(nt):
+                        w0 = u * (nt * nf // 4) + t * (nf // 4) + 128 * (i + g)
+                        c0 = 2 * n * g + u * n + 128 * t
+                        nc.tensor.transpose(bk[:, c0:c0 + 128], words[:, w0:w0 + 128], ident[:])
+            zb[(k, i)] = bk
+
+        def uc(k, i, eng):
+            (h, t0, nt, f0, nf) = UNITS[k]
+            n = 128 * nt
+            for g in range(2 // nt):
+                gg = f0 // 512 + i + g
+                if (h, gg) not in grp:
+                    gr = gpool.tile([P, 2048], BF16, name="gr%d" % (gg % 2), align_bytes=64)
+                    grp[(h, gg)] = gr
+                dst = grp[(h, gg)][:].bitcast(F32)[:, 256 * t0:256 * (t0 + nt)]
+                copy(eng, dst.rearrange("p (n u) -> p n u", u=2),
+                     zb[(k, i)][:, 2 * n * g:2 * n * (g + 1)].rearrange("p (u n) -> p n u", u=2))
+
+        zcodes = {}
+        zscales = {}
+
+        def uq(h, gg, t0=0, nt=4):
+            if (h, gg) not in zcodes:
+                zc = cpool.tile([P, 512], U32, name="zc", align_bytes=64)
+                zs = cpool.tile([P, 512], U8, name="zs", align_bytes=64)
+                zcodes[(h, gg)] = zc
+                zscales[(h, gg)] = zs
+            cols = slice(128 * t0, 128 * (t0 + nt))
+            nc.vector.quantize_mx(out=zcodes[(h, gg)][:, cols].bitcast(E5), scales=zscales[(h, gg)][:, cols],
+                                  in_=grp[(h, gg)][:, 512 * t0:512 * (t0 + nt)])
+
+        dphi = {}
+
+        def mx(h, g):
+            for s in range(4):
+                if g == 0:
+                    dphi[(h, s)] = bank(s)
+                nc.tensor.matmul_mx(
+                    out=dphi[(h, s)][:],
+                    lhsT=wcodes[g][:, 128 * s:128 * s + 128].bitcast(E4), lhsT_scale=wscales[g][:, 128 * s:128 * s + 128],
+                    rhs=zcodes[(h, g)][:].bitcast(E5), rhs_scale=zscales[(h, g)][:],
+                    start=(g == 0), stop=(g == 3))
+
+        acc = keep.tile([P, 8], F32, name="acc")
+        colsum = keep.tile([P, 4], F32, name="colsum")
+        tcodes = [keep.tile([P, 512], U32, name="tcodes%d" % h, align_bytes=64) for h in range(2)]
+        tscales = [keep.tile([P, 512], U8, name="tscales%d" % h, align_bytes=64) for h in range(2)]
+        ccodes = [keep.tile([P, 512], U32, name="ccodes%d" % h, align_bytes=64) for h in range(2)]
+        cscales = [keep.tile([P, 512], U8, name="cscales%d" % h, align_bytes=64) for h in range(2)]
+        tg = keep.tile([P, 2048], BF16, name="tg", align_bytes=64)
+        cg = keep.tile([P, 2048], BF16, name="cg", align_bytes=64)
+
+        def es(h, s):
+            nc.vector.scalar_tensor_tensor(out=ed[h][:, s, :], in0=dphi[(h, s)][:], scalar=twos2[:, s:s + 1],
+                                           in1=ed[h][:, s, :], op0=ALU.mult, op1=ALU.mult,
+                                           accum_out=acc[:, 4 * h + s:4 * h + s + 1])
+
+        eb = {}
+
+        def et(h, s, b):
+            bk = bank(b)
+            for t in range(4):
+                nc.tensor.transpose(bk[:, 128 * t:128 * t + 128], ed[h][:, s, 128 * t:128 * t + 128], ident[:])
+            eb[(h, s)] = bk
+
+        def ec(h, s, eng):
+            copy(eng, tg[:, 512 * s:512 * s + 512].rearrange("p (m t) -> p m t", t=4),
+                 eb[(h, s)][:].rearrange("p (t m) -> p m t", t=4))
+
+        def eq(h, s0, ns):
+            cols = slice(128 * s0, 128 * (s0 + ns))
+            nc.vector.quantize_mx(out=tcodes[h][:, cols].bitcast(E5), scales=tscales[h][:, cols], in_=tg[:, 512 * s0:512 * (s0 + ns)])
+
+        def il(h, t0, nt, eng):
+            copy(eng, cg[:, 512 * t0:512 * (t0 + nt)].rearrange("p (n s) -> p n s", s=4),
+                 ed[h][:, :, 128 * t0:128 * (t0 + nt)].rearrange("p s n -> p n s"))
+
+        def ilq(h, t0, nt):
+            cols = slice(128 * t0, 128 * (t0 + nt))
+            nc.vector.quantize_mx(out=ccodes[h][:, cols].bitcast(E5), scales=cscales[h][:, cols], in_=cg[:, 512 * t0:512 * (t0 + nt)])
+
+        rsum = [keep.tile([P, 4], F32, name="rsum%d" % h) for h in range(2)]
+        junk = keep.tile([P, 128], F32, name="junk")
+        rb = {}
+
+        def rm(h, b):
+            bk = bank(b)
+            for t in range(4):
+                for s in range(4):
+                    nc.tensor.matmul(bk[:, 128 * t:128 * t + 128], lhsT=ed[h][:, s, 128 * t:128 * t + 128], rhs=ident[:],
+                                     start=(s == 0), stop=(s == 3), is_transpose=True)
+            rb[h] = bk
+
+        def rr(h, eng):
+            if eng == "v":
+                nc.vector.tensor_reduce(out=rsum[h][:], in_=rb[h][:].rearrange("p (t m) -> p t m", t=4), axis=AX.X, op=ALU.add)
+            else:
+                for t in range(4):
+                    nc.scalar.activation(out=junk[:], in_=rb[h][:, 128 * t:128 * t + 128], func=ACT.Copy,
+                                         accum_out=rsum[h][:, t:t + 1])
+
+        o0 = [keep.tile([P, 4, IN], F32, name="o0_%d" % h) for h in range(2)]
+        o1 = keep.tile([P, 4, IN], F32, name="o1")
+        ob = {}
+
+        def o0m(h, t, b):
+            bk = bank(b)
+            cols = slice(128 * t, 128 * t + 128)
+            nc.tensor.matmul_mx(out=bk[:], lhsT=ccodes[h][:, cols].bitcast(E5), lhsT_scale=cscales[h][:, cols],
+                                rhs=rcodes[:, 128:640].bitcast(E4), rhs_scale=rscales[:, 128:640], start=True, stop=True)
+            ob[(h, t)] = bk
+
+        def o0f(h, t):
+            nc.vector.scalar_tensor_tensor(out=o0[h][:, t, :], in0=xneg[:, h, t, :], scalar=rsum[h][:, t:t + 1],
+                                           in1=ob[(h, t)][:, 0:128], op0=ALU.mult, op1=ALU.add)
+
+        def col():
+            nc.vector.tensor_tensor(out=colsum[:], in0=acc[:, 0:4], in1=acc[:, 4:8], op=ALU.add)
+
+        def o1m(s, h, b):
+            if h == 0:
+                ob[s] = bank(b)
+            cols = slice(128 * s, 128 * s + 128)
+            nc.tensor.matmul_mx(out=ob[s][:], lhsT=tcodes[h][:, cols].bitcast(E5), lhsT_scale=tscales[h][:, cols],
+                                rhs=rcodes[:, 256 * h:256 * h + 512].bitcast(E4),
+                                rhs_scale=rscales[:, 256 * h:256 * h + 512], start=(h == 0), stop=(h == 1))
+
+        def o1f(s):
+            nc.vector.scalar_tensor_tensor(out=o1[:, s, :], in0=cneg[:, s, :], scalar=colsum[:, s:s + 1],
+                                           in1=ob[s][:, 0:128], op0=ALU.mult, op1=ALU.add)
+
+        def st0(h, t0, nt):
+            nc.sync.dma_start(out=out_0[512 * h:512 * h + 512, :].rearrange("(p t) k -> p t k", t=4)[:, t0:t0 + nt, :],
+                              in_=o0[h][:, t0:t0 + nt, :])
+
+        def st1(s0, ns):
+            nc.sync.dma_start(out=out_1.rearrange("(m s) k -> m s k", s=4)[:, s0:s0 + ns, :], in_=o1[:, s0:s0 + ns, :])
+
+        load_w(1)
+        load_w(0)
+        wc(0, "v")
+        load_d(0)
+        db(0)
+        dt(0, 0, 6)
+        dt(0, 3, 7)
+        wq(0)
+        wc(1, "s")
+        wq(1)
+        load_c()
+        load_s()
+        sigma()
+        load_w(3)
+        load_w(2)
+        dt(0, 1, 3)
+        load_u(1)
+        load_u(0)
+        load_u(2)
+        load_u(3)
+        dx(0, 0)
+        wc(3, "v")
+        cc("s")
+        dx(0, 1)
+        load_d(1)
+        wq(3)
+        load_u(4)
+        load_u(5)
+        m(0)
+        ut(0, 0, 3)
+        wc(2, "s")
+        dx(0, 3)
+        dt(0, 2, 4)
+        wq(2)
+        m(1)
+        dx(0, 2)
+        rq(128, 128)
+        m(2)
+        m(3)
+        uc(0, 0, "s")
+        ut(2, 1, 3)
+        ut(1, 0, 1)
+        uc(1, 0, "s")
+        ut(2, 0, 4)
+        uc(2, 1, "s")
+        ut(3, 1, 2)
+        uc(3, 1, "s")
+        db(1)
+        load_u(7)
+        dt(1, 0, 3)
+        ut(3, 0, 1)
+        load_x()
+        dt(1, 1, 5)
+        uq(0, 1)
+        uc(2, 0, "s")
+        uq(0, 0)
+        dt(1, 2, 4)
+        m(4)
+        ut(4, 1, 7)
+        uc(4, 1, "v")
+        uc(3, 0, "s")
+        dx(1, 0)
+        uq(0, 3)
+        dx(1, 1)
+        ut(4, 0, 3)
+        uc(4, 0, "s")
+        uq(0, 2)
+        load_u(6)
+        mx(0, 0)
+        m(5)
+        mx(0, 1)
+        mx(0, 2)
+        mx(0, 3)
+        es(0, 0)
+        dx(1, 2)
+        ut(5, 0, 4)
+        uc(5, 0, "s")
+        ut(5, 1, 6)
+        uc(5, 1, "s")
+        et(0, 0, 4)
+        load_u(8)
+        es(0, 1)
+        es(0, 2)
+        et(0, 2, 5)
+        xc(1, "s")
+        ec(0, 0, "s")
+        es(0, 3)
+        et(0, 3, 2)
+        il(0, 0, 4, "s")
+        rm(0, 3)
+        m(7)
+        ut(7, 0, 4)
+        m(6)
+        uc(7, 0, "s")
+        ut(7, 1, 7)
+        ec(0, 2, "s")
+        ec(0, 3, "s")
+        ut(6, 0, 0)
+        dt(1, 3, 6)
+        uc(6, 0, "s")
+        uc(7, 1, "v")
+        et(0, 1, 5)
+        ut(6, 1, 1)
+        rr(0, "s")
+        m(8)
+        uq(1, 0)
+        uc(6, 1, "s")
+        ec(0, 1, "s")
+        rq(256, 128)
+        uq(1, 1)
+        ilq(0, 0, 4)
+        ut(8, 0, 7)
+        uc(8, 0, "s")
+        uq(1, 2)
+        neg()
+        ut(8, 1, 4)
+        eq(0, 0, 4)
+        uc(8, 1, "s")
+        mx(1, 0)
+        mx(1, 1)
+        uq(1, 3)
+        mx(1, 2)
+        mx(1, 3)
+        es(1, 0)
+        es(1, 1)
+        es(1, 2)
+        o0m(0, 3, 4)
+        xc(0, "s")
+        rq(0, 128)
+        dx(1, 3)
+        et(1, 0, 5)
+        ec(1, 0, "s")
+        et(1, 1, 7)
+        ec(1, 1, "s")
+        o0m(0, 1, 1)
+        es(1, 3)
+        il(1, 2, 2, "v")
+        il(1, 0, 2, "s")
+        et(1, 2, 6)
+        o0f(0, 3)
+        rm(1, 5)
+        et(1, 3, 0)
+        o0f(0, 1)
+        ec(1, 2, "s")
+        eq(1, 0, 2)
+        o0m(0, 2, 7)
+        o1m(1, 0, 1)
+        ilq(1, 2, 2)
+        o0m(1, 3, 3)
+        ec(1, 3, "v")
+        o1m(3, 0, 4)
+        o0m(0, 0, 0)
+        o0f(0, 2)
+        ilq(1, 0, 2)
+        o0m(1, 2, 6)
+        rr(1, "s")
+        o0f(1, 2)
+        o0f(1, 3)
+        eq(1, 2, 2)
+        o1m(1, 1, 1)
+        o0m(1, 0, 2)
+        o1m(2, 0, 5)
+        col()
+        o0f(1, 0)
+        o0f(0, 0)
+        st0(0, 0, 4)
+        o0m(1, 1, 6)
+        o0f(1, 1)
+        st0(1, 0, 4)
+        o1f(1)
+        o1m(3, 1, 4)
+        o1f(3)
+        o1m(0, 0, 3)
+        o1m(0, 1, 3)
+        o1f(0)
+        o1m(2, 1, 5)
+        o1f(2)
+        st1(0, 4)

@@ -18,13 +18,15 @@ ALU = mybir.AluOpType
 ACT = mybir.ActivationFunctionType
 AX = mybir.AxisListType
 P = 128
+BIG = 3.0e38
 
 UNITS = [
     (0, 0, 1, 0, 1024), (0, 1, 1, 0, 1024), (0, 2, 2, 0, 1024),
     (0, 0, 2, 1024, 1024), (0, 2, 2, 1024, 1024),
-    (1, 0, 2, 0, 1024), (1, 2, 2, 0, 1024),
-    (1, 0, 2, 1024, 1024), (1, 2, 2, 1024, 1024),
+    (1, 0, 2, 0, 1024), (1, 2, 2, 0, 1024), (1, 0, 2, 1024, 1024),
+    (1, 2, 1, 1024, 1024), (1, 3, 1, 1024, 512), (1, 3, 1, 1536, 512),
 ]
+SMASK = ()
 
 
 def tile_networkprc_pa_v_kernel(tc, x, centres, sigmas, w1, b1, d2, z2, grad_out, out_0, out_1):
@@ -46,10 +48,10 @@ def tile_networkprc_pa_v_kernel(tc, x, centres, sigmas, w1, b1, d2, z2, grad_out
         xraw = keep.tile([P, 2, 4, IN], BF16, name="xraw")
         wraw = [keep.tile([P, 4, HID], BF16, name="wraw%d" % g) for g in range(4)]
         draw = [keep.tile([P, 4, HID], F32, name="draw%d" % h) for h in range(2)]
-        zt = [keep.tile([P, u[2] * u[4]], F32, name="z%d" % k) for k, u in enumerate(UNITS[:7])]
-        gt = [keep.tile([P, u[2] * u[4]], BF16, name="g%d" % k) for k, u in enumerate(UNITS[:7])]
-        zt += zt[2:4]
-        gt += gt[2:4]
+        zt = [keep.tile([P, u[2] * u[4]], F32, name="z%d" % k)[:] for k, u in enumerate(UNITS[:7])]
+        gt = [keep.tile([P, u[2] * u[4]], BF16, name="g%d" % k)[:] for k, u in enumerate(UNITS[:7])]
+        for own in (zt, gt):
+            own += [own[2], own[0], own[1][:, 0:512], own[1][:, 512:1024]]
 
         def load_w(g):
             nc.sync.dma_start(out=wraw[g][:], in_=w1[512 * g:512 * g + 512, :].rearrange("(p j) c -> p j c", j=4))
@@ -61,7 +63,7 @@ def tile_networkprc_pa_v_kernel(tc, x, centres, sigmas, w1, b1, d2, z2, grad_out
             (h, t0, nt, f0, nf) = UNITS[k]
             for dst, src in ((zt[k], z2), (gt[k], grad_out)):
                 v = src[512 * h:512 * h + 512, f0:f0 + nf].rearrange("(p t) f -> p t f", t=4)[:, t0:t0 + nt, :]
-                nc.sync.dma_start(out=dst[:].rearrange("p (t f) -> p t f", t=nt), in_=v)
+                nc.sync.dma_start(out=dst.rearrange("p (t f) -> p t f", t=nt), in_=v)
 
         def load_s():
             nc.sync.dma_start(out=sg[:], in_=sigmas.rearrange("(p s) -> p s", s=4))
@@ -104,6 +106,8 @@ def tile_networkprc_pa_v_kernel(tc, x, centres, sigmas, w1, b1, d2, z2, grad_out
         def copy(eng, out, in_):
             if eng == "v":
                 nc.vector.tensor_copy(out=out, in_=in_)
+            elif eng == "g":
+                nc.gpsimd.tensor_scalar(out=out, in0=in_, scalar1=1.0, scalar2=1.0, op0=ALU.mult, op1=ALU.mult)
             else:
                 nc.scalar.copy(out=out, in_=in_)
 
@@ -120,10 +124,13 @@ def tile_networkprc_pa_v_kernel(tc, x, centres, sigmas, w1, b1, d2, z2, grad_out
         wscales = [keep.tile([P, HID], U8, name="wscales%d" % g, align_bytes=64) for g in range(4)]
         wgrp = {}
 
-        def wc(g, eng):
-            wg = gpool.tile([P, HID * 4], BF16, name="wg", align_bytes=64)
-            copy(eng, wg[:].rearrange("p (s m j) -> p s m j", s=4, j=4), wraw[g][:].rearrange("p j (m s) -> p s m j", s=4))
-            wgrp[g] = wg
+        def wc(g, hf, eng):
+            if g not in wgrp:
+                wg = gpool.tile([P, HID * 4], BF16, name="wg", align_bytes=64)
+                wgrp[g] = wg
+            cols = slice(1024 * hf, 1024 * hf + 1024)
+            copy(eng, wgrp[g][:, cols].rearrange("p (s m j) -> p s m j", s=2, j=4),
+                 wraw[g][:].rearrange("p j (m s) -> p s m j", s=4)[:, 2 * hf:2 * hf + 2])
 
         def wq(g):
             nc.vector.quantize_mx(out=wcodes[g][:].bitcast(E4), scales=wscales[g][:], in_=wgrp[g][:])
@@ -131,21 +138,18 @@ def tile_networkprc_pa_v_kernel(tc, x, centres, sigmas, w1, b1, d2, z2, grad_out
         ed = [keep.tile([P, 4, 512], F32, name="ed%d" % h) for h in range(2)]
         dT = {}
 
-        big = [keep.tile([P, 4, HID], F32, name="big%d" % h) for h in range(2)]
-
-        def db(h):
-            nc.vector.tensor_scalar(out=big[h][:], in0=draw[h][:], scalar1=0.0, scalar2=3.0e38, op0=ALU.is_le, op1=ALU.mult)
-
         def dt(h, s, b):
             bk = bank(b)
             for t in range(4):
-                cols = bk[:, 128 * t:128 * t + 128]
-                nc.tensor.matmul(cols, lhsT=draw[h][:, t, s:512:4], rhs=ident[:], start=True, stop=False, is_transpose=True)
-                nc.tensor.matmul(cols, lhsT=big[h][:, t, s:512:4], rhs=ident[:], start=False, stop=True, is_transpose=True)
+                nc.tensor.transpose(bk[:, 128 * t:128 * t + 128], draw[h][:, t, s:512:4], ident[:])
             dT[(h, s)] = bk
 
         def dx(h, s):
             nc.scalar.activation(out=ed[h][:, s, :], in_=dT[(h, s)][:], func=ACT.Exp, scale=negs2[:, s:s + 1])
+
+        def dm(h, s):
+            nc.vector.scalar_tensor_tensor(out=ed[h][:, s, :], in0=dT[(h, s)][:], scalar=0.0, in1=ed[h][:, s, :],
+                                           op0=ALU.is_gt, op1=ALU.mult)
 
         yt = {}
         grp = {}
@@ -154,8 +158,8 @@ def tile_networkprc_pa_v_kernel(tc, x, centres, sigmas, w1, b1, d2, z2, grad_out
             (h, t0, nt, f0, nf) = UNITS[k]
             y = ypool.tile([P, nt * nf], BF16, name="y")
             half = nt * nf // 2
-            zv = zt[k][:].rearrange("p (q u e) -> p u q e", u=2, e=2)
-            gv = gt[k][:].rearrange("p (q u e) -> p u q e", u=2, e=2)
+            zv = zt[k].rearrange("p (q u e) -> p u q e", u=2, e=2)
+            gv = gt[k].rearrange("p (q u e) -> p u q e", u=2, e=2)
             for u in range(2):
                 nc.vector.scalar_tensor_tensor(
                     out=y[:, u * half:(u + 1) * half].rearrange("p (q e) -> p q e", e=2),
@@ -169,18 +173,23 @@ def tile_networkprc_pa_v_kernel(tc, x, centres, sigmas, w1, b1, d2, z2, grad_out
             words = yt[k][:].bitcast(F32)
             n = 128 * nt
             bk = bank(b)
-            for g in range(2 // nt):
+            for g in range(min(2 // nt, nf // 512)):
                 for u in range(2):
                     for t in range(nt):
-                        w0 = u * (nt * nf // 4) + t * (nf // 4) + 128 * (i + g)
+                        if k in SMASK:
+                            w0 = t * (nf // 2) + 256 * (i + g) + u
+                            src = words[:, w0:w0 + 256:2]
+                        else:
+                            w0 = u * (nt * nf // 4) + t * (nf // 4) + 128 * (i + g)
+                            src = words[:, w0:w0 + 128]
                         c0 = 2 * n * g + u * n + 128 * t
-                        nc.tensor.transpose(bk[:, c0:c0 + 128], words[:, w0:w0 + 128], ident[:])
+                        nc.tensor.transpose(bk[:, c0:c0 + 128], src, ident[:])
             zb[(k, i)] = bk
 
         def uc(k, i, eng):
             (h, t0, nt, f0, nf) = UNITS[k]
             n = 128 * nt
-            for g in range(2 // nt):
+            for g in range(min(2 // nt, nf // 512)):
                 gg = f0 // 512 + i + g
                 if (h, gg) not in grp:
                     gr = gpool.tile([P, 2048], BF16, name="gr%d" % (gg % 2), align_bytes=64)
@@ -204,15 +213,14 @@ def tile_networkprc_pa_v_kernel(tc, x, centres, sigmas, w1, b1, d2, z2, grad_out
 
         dphi = {}
 
-        def mx(h, g):
-            for s in range(4):
-                if g == 0:
-                    dphi[(h, s)] = bank(s)
-                nc.tensor.matmul_mx(
-                    out=dphi[(h, s)][:],
-                    lhsT=wcodes[g][:, 128 * s:128 * s + 128].bitcast(E4), lhsT_scale=wscales[g][:, 128 * s:128 * s + 128],
-                    rhs=zcodes[(h, g)][:].bitcast(E5), rhs_scale=zscales[(h, g)][:],
-                    start=(g == 0), stop=(g == 3))
+        def mx(h, g, s, b=0):
+            if g == 0:
+                dphi[(h, s)] = bank(b)
+            nc.tensor.matmul_mx(
+                out=dphi[(h, s)][:],
+                lhsT=wcodes[g][:, 128 * s:128 * s + 128].bitcast(E4), lhsT_scale=wscales[g][:, 128 * s:128 * s + 128],
+                rhs=zcodes[(h, g)][:].bitcast(E5), rhs_scale=zscales[(h, g)][:],
+                start=(g == 0), stop=(g == 3))
 
         acc = keep.tile([P, 8], F32, name="acc")
         colsum = keep.tile([P, 4], F32, name="colsum")
@@ -309,181 +317,229 @@ def tile_networkprc_pa_v_kernel(tc, x, centres, sigmas, w1, b1, d2, z2, grad_out
         def st1(s0, ns):
             nc.sync.dma_start(out=out_1.rearrange("(m s) k -> m s k", s=4)[:, s0:s0 + ns, :], in_=o1[:, s0:s0 + ns, :])
 
-        load_w(1)
-        load_w(0)
-        wc(0, "v")
-        load_d(0)
-        db(0)
-        dt(0, 0, 6)
-        dt(0, 3, 7)
-        wq(0)
-        wc(1, "s")
-        wq(1)
-        load_c()
-        load_s()
-        sigma()
         load_w(3)
-        load_w(2)
-        dt(0, 1, 3)
-        load_u(1)
-        load_u(0)
+        load_w(0)
         load_u(2)
+        load_u(0)
+        load_w(1)
+        load_d(0)
+        load_s()
+        load_u(1)
         load_u(3)
-        dx(0, 0)
-        wc(3, "v")
-        cc("s")
-        dx(0, 1)
-        load_d(1)
-        wq(3)
         load_u(4)
-        load_u(5)
-        m(0)
-        ut(0, 0, 3)
-        wc(2, "s")
-        dx(0, 3)
-        dt(0, 2, 4)
-        wq(2)
-        m(1)
-        dx(0, 2)
-        rq(128, 128)
-        m(2)
-        m(3)
-        uc(0, 0, "s")
-        ut(2, 1, 3)
-        ut(1, 0, 1)
-        uc(1, 0, "s")
-        ut(2, 0, 4)
-        uc(2, 1, "s")
-        ut(3, 1, 2)
-        uc(3, 1, "s")
-        db(1)
-        load_u(7)
-        dt(1, 0, 3)
-        ut(3, 0, 1)
-        load_x()
-        dt(1, 1, 5)
-        uq(0, 1)
-        uc(2, 0, "s")
-        uq(0, 0)
-        dt(1, 2, 4)
-        m(4)
-        ut(4, 1, 7)
-        uc(4, 1, "v")
-        uc(3, 0, "s")
-        dx(1, 0)
-        uq(0, 3)
-        dx(1, 1)
-        ut(4, 0, 3)
-        uc(4, 0, "s")
-        uq(0, 2)
+        load_w(2)
+        load_d(1)
         load_u(6)
-        mx(0, 0)
-        m(5)
-        mx(0, 1)
-        mx(0, 2)
-        mx(0, 3)
-        es(0, 0)
-        dx(1, 2)
-        ut(5, 0, 4)
-        uc(5, 0, "s")
-        ut(5, 1, 6)
-        uc(5, 1, "s")
-        et(0, 0, 4)
+        load_c()
+        load_x()
+        load_u(5)
+        wc(3, 0, "s")
+        wc(0, 0, "s")
+        wc(0, 1, "s")
+        wc(3, 1, "s")
+        wq(0)
+        m(2)
+        ut(2, 0, 0)
+        m(0)
+        load_u(7)
+        ut(2, 1, 1)
+        wq(3)
+        ut(0, 0, 2)
         load_u(8)
-        es(0, 1)
-        es(0, 2)
-        et(0, 2, 5)
-        xc(1, "s")
-        ec(0, 0, "s")
-        es(0, 3)
-        et(0, 3, 2)
-        il(0, 0, 4, "s")
-        rm(0, 3)
-        m(7)
-        ut(7, 0, 4)
-        m(6)
-        uc(7, 0, "s")
-        ut(7, 1, 7)
-        ec(0, 2, "s")
-        ec(0, 3, "s")
-        ut(6, 0, 0)
-        dt(1, 3, 6)
-        uc(6, 0, "s")
-        uc(7, 1, "v")
-        et(0, 1, 5)
-        ut(6, 1, 1)
-        rr(0, "s")
-        m(8)
-        uq(1, 0)
-        uc(6, 1, "s")
-        ec(0, 1, "s")
-        rq(256, 128)
-        uq(1, 1)
-        ilq(0, 0, 4)
-        ut(8, 0, 7)
-        uc(8, 0, "s")
-        uq(1, 2)
-        neg()
-        ut(8, 1, 4)
-        eq(0, 0, 4)
-        uc(8, 1, "s")
-        mx(1, 0)
-        mx(1, 1)
-        uq(1, 3)
-        mx(1, 2)
-        mx(1, 3)
-        es(1, 0)
-        es(1, 1)
-        es(1, 2)
-        o0m(0, 3, 4)
-        xc(0, "s")
-        rq(0, 128)
+        wc(1, 0, "v")
+        wc(1, 1, "s")
+        dt(0, 1, 3)
+        sigma()
+        uc(0, 0, "s")
+        wq(1)
+        uc(2, 0, "s")
+        dt(0, 3, 4)
+        uc(2, 1, "v")
+        dx(0, 1)
+        dt(0, 0, 5)
+        m(1)
+        dx(0, 3)
+        ut(1, 0, 6)
+        dx(0, 0)
+        dm(0, 1)
+        load_u(9)
+        load_u(10)
+        dm(0, 3)
+        dt(0, 2, 7)
+        uc(1, 0, "s")
+        uq(0, 0)
+        dx(0, 2)
+        dm(0, 0)
+        mx(0, 0, 2, 2)
+        m(3)
+        mx(0, 0, 1, 0)
+        mx(0, 0, 0, 1)
+        mx(0, 0, 3, 3)
+        ut(3, 1, 4)
+        dm(0, 2)
+        ut(3, 0, 6)
+        uq(0, 1)
+        uc(3, 1, "s")
+        m(4)
+        mx(0, 1, 2)
+        uc(3, 0, "s")
+        mx(0, 1, 1)
+        mx(0, 1, 3)
+        mx(0, 1, 0)
+        wc(2, 0, "s")
+        ut(4, 1, 5)
+        wc(2, 1, "v")
+        ut(4, 0, 7)
+        wq(2)
+        uc(4, 1, "s")
+        dt(1, 3, 4)
+        uc(4, 0, "s")
+        uq(0, 3)
+        dt(1, 2, 6)
+        uq(0, 2)
         dx(1, 3)
-        et(1, 0, 5)
-        ec(1, 0, "s")
-        et(1, 1, 7)
-        ec(1, 1, "s")
-        o0m(0, 1, 1)
-        es(1, 3)
-        il(1, 2, 2, "v")
-        il(1, 0, 2, "s")
-        et(1, 2, 6)
-        o0f(0, 3)
-        rm(1, 5)
-        et(1, 3, 0)
+        dt(1, 1, 5)
+        dm(1, 3)
+        dx(1, 2)
+        mx(0, 2, 3)
+        dm(1, 2)
+        dx(1, 1)
+        mx(0, 2, 1)
+        mx(0, 2, 0)
+        mx(0, 3, 1)
+        m(6)
+        mx(0, 3, 0)
+        cc("s")
+        mx(0, 2, 2)
+        mx(0, 3, 2)
+        mx(0, 3, 3)
+        neg()
+        xc(1, "s")
+        dt(1, 0, 7)
+        ut(6, 1, 4)
+        rq(256, 128)
+        es(0, 0)
+        dx(1, 0)
+        ut(6, 0, 6)
+        es(0, 1)
+        et(0, 0, 1)
+        es(0, 2)
+        et(0, 1, 0)
+        es(0, 3)
+        xc(0, "g")
+        ec(0, 0, "s")
+        et(0, 2, 2)
+        m(5)
+        ec(0, 1, "s")
+        rm(0, 3)
+        il(0, 2, 1, "s")
+        ec(0, 2, "s")
+        il(0, 3, 1, "s")
+        rq(0, 128)
+        dm(1, 1)
+        il(0, 1, 1, "s")
+        ut(5, 1, 1)
+        m(7)
+        rr(0, "s")
+        ut(5, 0, 0)
+        uc(5, 1, "s")
+        et(0, 3, 2)
+        uc(5, 0, "s")
+        ut(7, 1, 5)
+        uc(6, 0, "s")
+        m(8)
+        uc(6, 1, "s")
+        ut(7, 0, 3)
+        uc(7, 1, "s")
+        uq(1, 0)
+        ut(8, 0, 1)
+        uc(7, 0, "s")
+        m(9)
+        mx(1, 0, 1, 0)
+        uc(8, 0, "s")
+        m(10)
+        mx(1, 0, 2, 6)
+        ut(9, 0, 4)
+        il(0, 0, 1, "s")
+        rq(128, 128)
+        ut(10, 0, 5)
+        uq(1, 1)
+        mx(1, 0, 0, 3)
+        uc(9, 0, "s")
+        ilq(0, 0, 4)
+        mx(1, 0, 3, 1)
+        uc(10, 0, "s")
+        mx(1, 1, 1)
+        mx(1, 1, 3)
+        uq(1, 2)
+        o0m(0, 1, 4)
+        mx(1, 1, 0)
+        uq(1, 3, 0, 2)
+        o0m(0, 0, 5)
+        uq(1, 3, 2, 1)
+        mx(1, 2, 1)
+        uq(1, 3, 3, 1)
         o0f(0, 1)
-        ec(1, 2, "s")
-        eq(1, 0, 2)
-        o0m(0, 2, 7)
-        o1m(1, 0, 1)
-        ilq(1, 2, 2)
-        o0m(1, 3, 3)
-        ec(1, 3, "v")
-        o1m(3, 0, 4)
-        o0m(0, 0, 0)
+        mx(1, 1, 2)
+        ec(0, 3, "v")
+        mx(1, 3, 1)
+        o0m(0, 3, 4)
+        dm(1, 0)
+        mx(1, 2, 0)
+        mx(1, 3, 0)
+        eq(0, 0, 4)
+        mx(1, 2, 2)
+        mx(1, 3, 2)
+        o0m(0, 2, 2)
+        o0f(0, 3)
+        es(1, 0)
+        o1m(2, 0, 7)
+        o1m(1, 0, 4)
+        mx(1, 2, 3)
+        es(1, 1)
+        mx(1, 3, 3)
+        et(1, 0, 3)
+        es(1, 2)
+        et(1, 1, 0)
+        es(1, 3)
+        ec(1, 0, "s")
+        et(1, 2, 6)
         o0f(0, 2)
-        ilq(1, 0, 2)
-        o0m(1, 2, 6)
-        rr(1, "s")
-        o0f(1, 2)
-        o0f(1, 3)
-        eq(1, 2, 2)
-        o1m(1, 1, 1)
-        o0m(1, 0, 2)
-        o1m(2, 0, 5)
+        il(1, 1, 1, "v")
+        ec(1, 1, "s")
+        eq(1, 0, 1)
+        et(1, 3, 1)
         col()
-        o0f(1, 0)
+        il(1, 3, 1, "v")
+        ec(1, 2, "v")
+        o1m(3, 0, 2)
+        ec(1, 3, "s")
+        o1m(0, 0, 3)
+        il(1, 0, 1, "v")
+        o1m(0, 1, 3)
+        il(1, 2, 1, "v")
+        rm(1, 0)
+        ilq(1, 0, 2)
+        ilq(1, 2, 2)
+        o1f(0)
+        eq(1, 2, 2)
+        rr(1, "s")
         o0f(0, 0)
+        eq(1, 1, 1)
         st0(0, 0, 4)
         o0m(1, 1, 6)
+        o0m(1, 3, 1)
+        o0m(1, 0, 3)
         o0f(1, 1)
-        st0(1, 0, 4)
+        o0m(1, 2, 5)
+        o0f(1, 3)
+        o1m(1, 1, 4)
+        o0f(1, 0)
+        o1m(3, 1, 2)
+        o0f(1, 2)
+        o1m(2, 1, 7)
         o1f(1)
-        o1m(3, 1, 4)
+        st0(1, 0, 4)
         o1f(3)
-        o1m(0, 0, 3)
-        o1m(0, 1, 3)
-        o1f(0)
-        o1m(2, 1, 5)
         o1f(2)
         st1(0, 4)

@@ -318,228 +318,230 @@ def tile_networkprc_pa_v_kernel(tc, x, centres, sigmas, w1, b1, d2, z2, grad_out
             nc.sync.dma_start(out=out_1.rearrange("(m s) k -> m s k", s=4)[:, s0:s0 + ns, :], in_=o1[:, s0:s0 + ns, :])
 
         load_w(3)
-        load_w(0)
-        load_u(2)
-        load_u(0)
+        load_s()
         load_w(1)
         load_d(0)
-        load_s()
+        load_u(2)
+        load_w(0)
+        load_u(0)
         load_u(1)
         load_u(3)
         load_u(4)
         load_w(2)
-        load_d(1)
-        load_u(6)
-        load_c()
         load_x()
+        load_d(1)
         load_u(5)
+        load_c()
+        load_u(6)
         wc(3, 0, "s")
-        wc(0, 0, "s")
-        wc(0, 1, "s")
-        wc(3, 1, "s")
-        wq(0)
-        m(2)
-        ut(2, 0, 0)
-        m(0)
-        load_u(7)
-        ut(2, 1, 1)
-        wq(3)
-        ut(0, 0, 2)
-        load_u(8)
-        wc(1, 0, "v")
-        wc(1, 1, "s")
-        dt(0, 1, 3)
         sigma()
-        uc(0, 0, "s")
+        wc(1, 0, "s")
+        wc(1, 1, "v")
+        wc(3, 1, "s")
         wq(1)
-        uc(2, 0, "s")
-        dt(0, 3, 4)
-        uc(2, 1, "v")
+        dt(0, 1, 0)
+        wq(3)
+        dt(0, 2, 1)
         dx(0, 1)
-        dt(0, 0, 5)
-        m(1)
-        dx(0, 3)
-        ut(1, 0, 6)
-        dx(0, 0)
+        dt(0, 3, 2)
+        dt(0, 0, 3)
+        dx(0, 2)
         dm(0, 1)
-        load_u(9)
-        load_u(10)
+        dx(0, 3)
+        dm(0, 2)
+        dx(0, 0)
         dm(0, 3)
-        dt(0, 2, 7)
+        m(2)
+        wc(0, 0, "s")
+        ut(2, 1, 4)
+        wc(0, 1, "v")
+        load_u(7)
+        ut(2, 0, 5)
+        m(0)
+        ut(0, 0, 6)
+        wq(0)
+        load_u(8)
+        m(1)
+        uc(0, 0, "s")
+        uc(2, 0, "s")
+        ut(1, 0, 7)
+        dm(0, 0)
+        load_u(10)
+        load_u(9)
+        uc(2, 1, "v")
         uc(1, 0, "s")
         uq(0, 0)
-        dx(0, 2)
-        dm(0, 0)
-        mx(0, 0, 2, 2)
-        m(3)
-        mx(0, 0, 1, 0)
-        mx(0, 0, 0, 1)
-        mx(0, 0, 3, 3)
-        ut(3, 1, 4)
-        dm(0, 2)
-        ut(3, 0, 6)
         uq(0, 1)
-        uc(3, 1, "s")
-        m(4)
-        mx(0, 1, 2)
-        uc(3, 0, "s")
-        mx(0, 1, 1)
-        mx(0, 1, 3)
+        mx(0, 0, 0, 0)
+        m(3)
+        mx(0, 0, 2, 1)
         mx(0, 1, 0)
+        mx(0, 0, 1, 2)
+        mx(0, 1, 1)
+        mx(0, 1, 2)
+        ut(3, 0, 6)
+        ut(3, 1, 5)
+        m(4)
+        uc(3, 0, "s")
+        mx(0, 0, 3, 3)
+        mx(0, 1, 3)
+        uc(3, 1, "s")
+        ut(4, 0, 4)
         wc(2, 0, "s")
-        ut(4, 1, 5)
+        neg()
+        xc(1, "v")
         wc(2, 1, "v")
-        ut(4, 0, 7)
+        xc(0, "s")
+        ut(4, 1, 7)
+        rq(256, 128)
+        uc(4, 0, "s")
+        rq(0, 128)
         wq(2)
         uc(4, 1, "s")
-        dt(1, 3, 4)
-        uc(4, 0, "s")
-        uq(0, 3)
-        dt(1, 2, 6)
+        dt(1, 0, 6)
         uq(0, 2)
+        dt(1, 3, 5)
+        uq(0, 3)
+        dx(1, 0)
+        dt(1, 1, 4)
+        mx(0, 2, 0)
         dx(1, 3)
-        dt(1, 1, 5)
-        dm(1, 3)
-        dx(1, 2)
-        mx(0, 2, 3)
-        dm(1, 2)
+        dm(1, 0)
+        mx(0, 3, 0)
         dx(1, 1)
         mx(0, 2, 1)
-        mx(0, 2, 0)
+        dm(1, 3)
         mx(0, 3, 1)
-        m(6)
-        mx(0, 3, 0)
-        cc("s")
         mx(0, 2, 2)
-        mx(0, 3, 2)
-        mx(0, 3, 3)
-        neg()
-        xc(1, "s")
-        dt(1, 0, 7)
-        ut(6, 1, 4)
-        rq(256, 128)
         es(0, 0)
-        dx(1, 0)
-        ut(6, 0, 6)
+        mx(0, 3, 2)
+        mx(0, 2, 3)
+        mx(0, 3, 3)
         es(0, 1)
-        et(0, 0, 1)
+        cc("s")
+        et(0, 0, 7)
         es(0, 2)
-        et(0, 1, 0)
-        es(0, 3)
-        xc(0, "g")
-        ec(0, 0, "s")
-        et(0, 2, 2)
-        m(5)
-        ec(0, 1, "s")
-        rm(0, 3)
-        il(0, 2, 1, "s")
-        ec(0, 2, "s")
-        il(0, 3, 1, "s")
-        rq(0, 128)
-        dm(1, 1)
-        il(0, 1, 1, "s")
-        ut(5, 1, 1)
-        m(7)
-        rr(0, "s")
-        ut(5, 0, 0)
-        uc(5, 1, "s")
-        et(0, 3, 2)
-        uc(5, 0, "s")
-        ut(7, 1, 5)
-        uc(6, 0, "s")
-        m(8)
-        uc(6, 1, "s")
-        ut(7, 0, 3)
-        uc(7, 1, "s")
-        uq(1, 0)
-        ut(8, 0, 1)
-        uc(7, 0, "s")
-        m(9)
-        mx(1, 0, 1, 0)
-        uc(8, 0, "s")
-        m(10)
-        mx(1, 0, 2, 6)
-        ut(9, 0, 4)
-        il(0, 0, 1, "s")
+        et(0, 1, 6)
         rq(128, 128)
-        ut(10, 0, 5)
-        uq(1, 1)
-        mx(1, 0, 0, 3)
-        uc(9, 0, "s")
+        ec(0, 0, "s")
+        es(0, 3)
+        et(0, 2, 5)
+        ec(0, 1, "s")
+        dt(1, 2, 0)
+        m(5)
+        il(0, 0, 1, "s")
+        et(0, 3, 2)
+        rm(0, 1)
+        dx(1, 2)
+        il(0, 1, 1, "s")
+        il(0, 3, 1, "s")
+        m(6)
+        il(0, 2, 1, "s")
+        ut(5, 0, 7)
+        ut(5, 1, 3)
+        rr(0, "s")
+        ut(6, 0, 6)
+        uc(5, 0, "s")
         ilq(0, 0, 4)
-        mx(1, 0, 3, 1)
-        uc(10, 0, "s")
-        mx(1, 1, 1)
-        mx(1, 1, 3)
-        uq(1, 2)
-        o0m(0, 1, 4)
-        mx(1, 1, 0)
-        uq(1, 3, 0, 2)
-        o0m(0, 0, 5)
-        uq(1, 3, 2, 1)
-        mx(1, 2, 1)
-        uq(1, 3, 3, 1)
+        ec(0, 2, "s")
+        ut(6, 1, 1)
+        m(7)
+        uc(5, 1, "s")
+        o0m(0, 2, 7)
+        uc(6, 0, "s")
+        o0m(0, 1, 5)
+        o0m(0, 3, 3)
+        uc(6, 1, "s")
+        ut(7, 1, 6)
+        ec(0, 3, "s")
+        uq(1, 0)
+        ut(7, 0, 1)
+        o0f(0, 3)
         o0f(0, 1)
+        uc(7, 1, "s")
+        uq(1, 1)
+        mx(1, 0, 2, 2)
+        mx(1, 0, 0, 3)
+        uc(7, 0, "s")
+        m(8)
+        mx(1, 0, 3, 5)
+        mx(1, 1, 3)
+        mx(1, 1, 0)
+        ut(8, 0, 6)
+        m(9)
+        uq(1, 3, 0, 2)
+        ut(9, 0, 1)
+        uc(8, 0, "s")
+        o0f(0, 2)
         mx(1, 1, 2)
-        ec(0, 3, "v")
-        mx(1, 3, 1)
-        o0m(0, 3, 4)
-        dm(1, 0)
+        m(10)
+        mx(1, 0, 1, 7)
+        uc(9, 0, "s")
+        mx(1, 1, 1)
+        uq(1, 3, 2, 1)
+        ut(10, 0, 6)
+        uq(1, 2)
+        o0m(0, 0, 1)
+        dm(1, 2)
+        uc(10, 0, "s")
+        mx(1, 2, 1)
+        mx(1, 2, 3)
+        o0f(0, 0)
+        uq(1, 3, 3, 1)
+        mx(1, 2, 2)
+        eq(0, 0, 4)
+        st0(0, 0, 4)
         mx(1, 2, 0)
         mx(1, 3, 0)
-        eq(0, 0, 4)
-        mx(1, 2, 2)
+        dm(1, 1)
+        mx(1, 3, 1)
+        o1m(0, 0, 6)
         mx(1, 3, 2)
-        o0m(0, 2, 2)
-        o0f(0, 3)
         es(1, 0)
-        o1m(2, 0, 7)
-        o1m(1, 0, 4)
-        mx(1, 2, 3)
-        es(1, 1)
         mx(1, 3, 3)
-        et(1, 0, 3)
+        o1m(2, 0, 0)
+        es(1, 1)
+        o1m(1, 0, 1)
+        o1m(3, 0, 4)
         es(1, 2)
-        et(1, 1, 0)
+        et(1, 0, 3)
+        et(1, 1, 7)
         es(1, 3)
         ec(1, 0, "s")
-        et(1, 2, 6)
-        o0f(0, 2)
-        il(1, 1, 1, "v")
-        ec(1, 1, "s")
-        eq(1, 0, 1)
-        et(1, 3, 1)
+        et(1, 2, 2)
         col()
-        il(1, 3, 1, "v")
-        ec(1, 2, "v")
-        o1m(3, 0, 2)
-        ec(1, 3, "s")
-        o1m(0, 0, 3)
+        et(1, 3, 5)
+        il(1, 1, 1, "v")
+        il(1, 3, 1, "s")
         il(1, 0, 1, "v")
-        o1m(0, 1, 3)
+        rm(1, 3)
+        ec(1, 2, "s")
         il(1, 2, 1, "v")
-        rm(1, 0)
         ilq(1, 0, 2)
+        ec(1, 1, "s")
         ilq(1, 2, 2)
-        o1f(0)
-        eq(1, 2, 2)
+        ec(1, 3, "v")
         rr(1, "s")
-        o0f(0, 0)
         eq(1, 1, 1)
-        st0(0, 0, 4)
-        o0m(1, 1, 6)
-        o0m(1, 3, 1)
-        o0m(1, 0, 3)
-        o0f(1, 1)
+        o0m(1, 3, 2)
+        eq(1, 2, 2)
+        o0m(1, 0, 7)
+        eq(1, 0, 1)
         o0m(1, 2, 5)
         o0f(1, 3)
-        o1m(1, 1, 4)
+        o1m(1, 1, 1)
         o0f(1, 0)
-        o1m(3, 1, 2)
+        o0m(1, 1, 3)
         o0f(1, 2)
-        o1m(2, 1, 7)
+        o1m(0, 1, 6)
         o1f(1)
-        st0(1, 0, 4)
-        o1f(3)
+        o1m(2, 1, 0)
+        st0(1, 2, 2)
+        o0f(1, 1)
+        o1m(3, 1, 4)
+        o1f(0)
+        st0(1, 0, 2)
         o1f(2)
-        st1(0, 4)
+        st1(0, 2)
+        o1f(3)
+        st1(2, 2)

from contextlib import ExitStack

import concourse.mybir as mybir
from concourse.masks import make_identity

B, IN, HID, CENT = 1024, 128, 512, 2048
FLOPS = 2 * B * CENT * HID + 2 * 2 * B * HID * IN
BYTES = (B * CENT * 6 + B * HID * 4 + CENT * HID * 2 + B * IN * 2 + HID * IN * 2
         + HID * 2 + B * IN * 4 + HID * IN * 4)

F32 = mybir.dt.float32
BF16 = mybir.dt.bfloat16
U32 = mybir.dt.uint32
U8 = mybir.dt.uint8
E4 = mybir.dt.float8_e4m3fn_x4
E5 = mybir.dt.float8_e5m2_x4
ALU = mybir.AluOpType
ACT = mybir.ActivationFunctionType
AX = mybir.AxisListType
P = 128
BIG = 3.0e38

UNITS = [
    (0, 0, 1, 0, 1024), (0, 1, 1, 0, 1024), (0, 2, 2, 0, 1024),
    (0, 0, 2, 1024, 1024), (0, 2, 2, 1024, 1024),
    (1, 0, 2, 0, 1024), (1, 2, 2, 0, 1024), (1, 0, 2, 1024, 1024),
    (1, 2, 1, 1024, 1024), (1, 3, 1, 1024, 512), (1, 3, 1, 1536, 512),
]
SMASK = ()


def tile_networkprc_pa_v_kernel(tc, x, centres, sigmas, w1, b1, d2, z2, grad_out, out_0, out_1):
    nc = tc.nc
    with ExitStack() as ctx:
        keep = ctx.enter_context(tc.tile_pool(name="keep", bufs=1))
        ypool = ctx.enter_context(tc.tile_pool(name="ypool", bufs=3))
        gpool = ctx.enter_context(tc.tile_pool(name="gpool", bufs=2))
        cpool = ctx.enter_context(tc.tile_pool(name="cpool", bufs=4))
        psum = ctx.enter_context(tc.psum_pool(name="psum", bufs=1))
        ctx.enter_context(tc.manual_schedule())

        def bank(i):
            b = psum.tile([P, 512], F32, name="bank%d" % i)
            return b

        sg = keep.tile([P, 4], BF16, name="sg")
        craw = keep.tile([P, 4, IN], BF16, name="craw")
        xraw = keep.tile([P, 2, 4, IN], BF16, name="xraw")
        wraw = [keep.tile([P, 4, HID], BF16, name="wraw%d" % g) for g in range(4)]
        draw = [keep.tile([P, 4, HID], F32, name="draw%d" % h) for h in range(2)]
        zt = [keep.tile([P, u[2] * u[4]], F32, name="z%d" % k)[:] for k, u in enumerate(UNITS[:7])]
        gt = [keep.tile([P, u[2] * u[4]], BF16, name="g%d" % k)[:] for k, u in enumerate(UNITS[:7])]
        for own in (zt, gt):
            own += [own[2], own[0], own[1][:, 0:512], own[1][:, 512:1024]]

        def load_w(g):
            nc.sync.dma_start(out=wraw[g][:], in_=w1[512 * g:512 * g + 512, :].rearrange("(p j) c -> p j c", j=4))

        def load_d(h):
            nc.sync.dma_start(out=draw[h][:], in_=d2[512 * h:512 * h + 512, :].rearrange("(p t) c -> p t c", t=4))

        def load_u(k):
            (h, t0, nt, f0, nf) = UNITS[k]
            for dst, src in ((zt[k], z2), (gt[k], grad_out)):
                v = src[512 * h:512 * h + 512, f0:f0 + nf].rearrange("(p t) f -> p t f", t=4)[:, t0:t0 + nt, :]
                nc.sync.dma_start(out=dst.rearrange("p (t f) -> p t f", t=nt), in_=v)

        def load_s():
            nc.sync.dma_start(out=sg[:], in_=sigmas.rearrange("(p s) -> p s", s=4))

        def load_c():
            nc.sync.dma_start(out=craw[:], in_=centres.rearrange("(p j) k -> p j k", j=4))

        def load_x():
            nc.sync.dma_start(out=xraw[:], in_=x.rearrange("(h p j) k -> p h j k", h=2, j=4))

        one = keep.tile([P, 1], F32, name="one")
        nc.gpsimd.memset(one[:], 1.0)
        ident = keep.tile([P, P], F32, name="ident")
        make_identity(nc, ident[:])
        warm = keep.tile([P, 1], F32, name="warm")
        nc.scalar.activation(out=warm[:], in_=one[:], func=ACT.Exp)
        rcodes = keep.tile([P, 768], U32, name="rcodes", align_bytes=64)
        rscales = keep.tile([P, 768], U8, name="rscales", align_bytes=64)
        nc.gpsimd.memset(rcodes[:, 384:768], 0)
        nc.gpsimd.memset(rscales[:, 384:768], 0)
        s2 = keep.tile([P, 4], F32, name="s2")
        negs2 = keep.tile([P, 4], F32, name="negs2")
        twos2 = keep.tile([P, 4], F32, name="twos2")

        xneg = keep.tile([P, 2, 4, IN], BF16, name="xneg")
        cneg = keep.tile([P, 4, IN], BF16, name="cneg")

        def neg():
            nc.gpsimd.tensor_scalar(out=xneg[:], in0=xraw[:], scalar1=-1.0, scalar2=0.0, op0=ALU.mult, op1=ALU.add)
            nc.gpsimd.tensor_scalar(out=cneg[:], in0=craw[:], scalar1=-1.0, scalar2=0.0, op0=ALU.mult, op1=ALU.add)

        def sigma():
            nc.vector.tensor_tensor(out=s2[:], in0=sg[:], in1=sg[:], op=ALU.mult)
            nc.vector.tensor_scalar(out=negs2[:], in0=s2[:], scalar1=-1.0, scalar2=None, op0=ALU.mult)
            nc.vector.tensor_scalar(out=twos2[:], in0=s2[:], scalar1=2.0, scalar2=None, op0=ALU.mult)

        rgrp = keep.tile([P, 384, 4], BF16, name="rgrp", align_bytes=64)
        rflat = rgrp[:].rearrange("p k j -> p (k j)")

        def copy(eng, out, in_):
            if eng == "v":
                nc.vector.tensor_copy(out=out, in_=in_)
            elif eng == "g":
                nc.gpsimd.tensor_scalar(out=out, in0=in_, scalar1=1.0, scalar2=1.0, op0=ALU.mult, op1=ALU.mult)
            else:
                nc.scalar.copy(out=out, in_=in_)

        def cc(eng):
            copy(eng, rgrp[:, 128:256, :], craw[:].rearrange("p j k -> p k j"))

        def xc(h, eng):
            copy(eng, rgrp[:, 256 * h:256 * h + 128, :], xraw[:, h].rearrange("p j k -> p k j"))

        def rq(w0, n):
            nc.vector.quantize_mx(out=rcodes[:, w0:w0 + n].bitcast(E4), scales=rscales[:, w0:w0 + n], in_=rflat[:, 4 * w0:4 * (w0 + n)])

        wcodes = [keep.tile([P, HID], U32, name="wcodes%d" % g, align_bytes=64) for g in range(4)]
        wscales = [keep.tile([P, HID], U8, name="wscales%d" % g, align_bytes=64) for g in range(4)]
        wgrp = {}

        def wc(g, hf, eng):
            if g not in wgrp:
                wg = gpool.tile([P, HID * 4], BF16, name="wg", align_bytes=64)
                wgrp[g] = wg
            cols = slice(1024 * hf, 1024 * hf + 1024)
            copy(eng, wgrp[g][:, cols].rearrange("p (s m j) -> p s m j", s=2, j=4),
                 wraw[g][:].rearrange("p j (m s) -> p s m j", s=4)[:, 2 * hf:2 * hf + 2])

        def wq(g):
            nc.vector.quantize_mx(out=wcodes[g][:].bitcast(E4), scales=wscales[g][:], in_=wgrp[g][:])

        ed = [keep.tile([P, 4, 512], F32, name="ed%d" % h) for h in range(2)]
        dT = {}

        def dt(h, s, b):
            bk = bank(b)
            for t in range(4):
                nc.tensor.transpose(bk[:, 128 * t:128 * t + 128], draw[h][:, t, s:512:4], ident[:])
            dT[(h, s)] = bk

        def dx(h, s):
            nc.scalar.activation(out=ed[h][:, s, :], in_=dT[(h, s)][:], func=ACT.Exp, scale=negs2[:, s:s + 1])

        def dm(h, s):
            nc.vector.scalar_tensor_tensor(out=ed[h][:, s, :], in0=dT[(h, s)][:], scalar=0.0, in1=ed[h][:, s, :],
                                           op0=ALU.is_gt, op1=ALU.mult)

        yt = {}
        grp = {}

        def m(k):
            (h, t0, nt, f0, nf) = UNITS[k]
            y = ypool.tile([P, nt * nf], BF16, name="y")
            half = nt * nf // 2
            zv = zt[k].rearrange("p (q u e) -> p u q e", u=2, e=2)
            gv = gt[k].rearrange("p (q u e) -> p u q e", u=2, e=2)
            for u in range(2):
                nc.vector.scalar_tensor_tensor(
                    out=y[:, u * half:(u + 1) * half].rearrange("p (q e) -> p q e", e=2),
                    in0=zv[:, u], scalar=0.0, in1=gv[:, u], op0=ALU.is_gt, op1=ALU.mult)
            yt[k] = y

        zb = {}

        def ut(k, i, b):
            (h, t0, nt, f0, nf) = UNITS[k]
            words = yt[k][:].bitcast(F32)
            n = 128 * nt
            bk = bank(b)
            for g in range(min(2 // nt, nf // 512)):
                for u in range(2):
                    for t in range(nt):
                        if k in SMASK:
                            w0 = t * (nf // 2) + 256 * (i + g) + u
                            src = words[:, w0:w0 + 256:2]
                        else:
                            w0 = u * (nt * nf // 4) + t * (nf // 4) + 128 * (i + g)
                            src = words[:, w0:w0 + 128]
                        c0 = 2 * n * g + u * n + 128 * t
                        nc.tensor.transpose(bk[:, c0:c0 + 128], src, ident[:])
            zb[(k, i)] = bk

        def uc(k, i, eng):
            (h, t0, nt, f0, nf) = UNITS[k]
            n = 128 * nt
            for g in range(min(2 // nt, nf // 512)):
                gg = f0 // 512 + i + g
                if (h, gg) not in grp:
                    gr = gpool.tile([P, 2048], BF16, name="gr%d" % (gg % 2), align_bytes=64)
                    grp[(h, gg)] = gr
                dst = grp[(h, gg)][:].bitcast(F32)[:, 256 * t0:256 * (t0 + nt)]
                copy(eng, dst.rearrange("p (n u) -> p n u", u=2),
                     zb[(k, i)][:, 2 * n * g:2 * n * (g + 1)].rearrange("p (u n) -> p n u", u=2))

        zcodes = {}
        zscales = {}

        def uq(h, gg, t0=0, nt=4):
            if (h, gg) not in zcodes:
                zc = cpool.tile([P, 512], U32, name="zc", align_bytes=64)
                zs = cpool.tile([P, 512], U8, name="zs", align_bytes=64)
                zcodes[(h, gg)] = zc
                zscales[(h, gg)] = zs
            cols = slice(128 * t0, 128 * (t0 + nt))
            nc.vector.quantize_mx(out=zcodes[(h, gg)][:, cols].bitcast(E5), scales=zscales[(h, gg)][:, cols],
                                  in_=grp[(h, gg)][:, 512 * t0:512 * (t0 + nt)])

        dphi = {}

        def mx(h, g, s, b=0):
            if g == 0:
                dphi[(h, s)] = bank(b)
            nc.tensor.matmul_mx(
                out=dphi[(h, s)][:],
                lhsT=wcodes[g][:, 128 * s:128 * s + 128].bitcast(E4), lhsT_scale=wscales[g][:, 128 * s:128 * s + 128],
                rhs=zcodes[(h, g)][:].bitcast(E5), rhs_scale=zscales[(h, g)][:],
                start=(g == 0), stop=(g == 3))

        acc = keep.tile([P, 8], F32, name="acc")
        colsum = keep.tile([P, 4], F32, name="colsum")
        tcodes = [keep.tile([P, 512], U32, name="tcodes%d" % h, align_bytes=64) for h in range(2)]
        tscales = [keep.tile([P, 512], U8, name="tscales%d" % h, align_bytes=64) for h in range(2)]
        ccodes = [keep.tile([P, 512], U32, name="ccodes%d" % h, align_bytes=64) for h in range(2)]
        cscales = [keep.tile([P, 512], U8, name="cscales%d" % h, align_bytes=64) for h in range(2)]
        tg = keep.tile([P, 2048], BF16, name="tg", align_bytes=64)
        cg = keep.tile([P, 2048], BF16, name="cg", align_bytes=64)

        def es(h, s):
            nc.vector.scalar_tensor_tensor(out=ed[h][:, s, :], in0=dphi[(h, s)][:], scalar=twos2[:, s:s + 1],
                                           in1=ed[h][:, s, :], op0=ALU.mult, op1=ALU.mult,
                                           accum_out=acc[:, 4 * h + s:4 * h + s + 1])

        eb = {}

        def et(h, s, b):
            bk = bank(b)
            for t in range(4):
                nc.tensor.transpose(bk[:, 128 * t:128 * t + 128], ed[h][:, s, 128 * t:128 * t + 128], ident[:])
            eb[(h, s)] = bk

        def ec(h, s, eng):
            copy(eng, tg[:, 512 * s:512 * s + 512].rearrange("p (m t) -> p m t", t=4),
                 eb[(h, s)][:].rearrange("p (t m) -> p m t", t=4))

        def eq(h, s0, ns):
            cols = slice(128 * s0, 128 * (s0 + ns))
            nc.vector.quantize_mx(out=tcodes[h][:, cols].bitcast(E5), scales=tscales[h][:, cols], in_=tg[:, 512 * s0:512 * (s0 + ns)])

        def il(h, t0, nt, eng):
            copy(eng, cg[:, 512 * t0:512 * (t0 + nt)].rearrange("p (n s) -> p n s", s=4),
                 ed[h][:, :, 128 * t0:128 * (t0 + nt)].rearrange("p s n -> p n s"))

        def ilq(h, t0, nt):
            cols = slice(128 * t0, 128 * (t0 + nt))
            nc.vector.quantize_mx(out=ccodes[h][:, cols].bitcast(E5), scales=cscales[h][:, cols], in_=cg[:, 512 * t0:512 * (t0 + nt)])

        rsum = [keep.tile([P, 4], F32, name="rsum%d" % h) for h in range(2)]
        junk = keep.tile([P, 128], F32, name="junk")
        rb = {}

        def rm(h, b):
            bk = bank(b)
            for t in range(4):
                for s in range(4):
                    nc.tensor.matmul(bk[:, 128 * t:128 * t + 128], lhsT=ed[h][:, s, 128 * t:128 * t + 128], rhs=ident[:],
                                     start=(s == 0), stop=(s == 3), is_transpose=True)
            rb[h] = bk

        def rr(h, eng):
            if eng == "v":
                nc.vector.tensor_reduce(out=rsum[h][:], in_=rb[h][:].rearrange("p (t m) -> p t m", t=4), axis=AX.X, op=ALU.add)
            else:
                for t in range(4):
                    nc.scalar.activation(out=junk[:], in_=rb[h][:, 128 * t:128 * t + 128], func=ACT.Copy,
                                         accum_out=rsum[h][:, t:t + 1])

        o0 = [keep.tile([P, 4, IN], F32, name="o0_%d" % h) for h in range(2)]
        o1 = keep.tile([P, 4, IN], F32, name="o1")
        ob = {}

        def o0m(h, t, b):
            bk = bank(b)
            cols = slice(128 * t, 128 * t + 128)
            nc.tensor.matmul_mx(out=bk[:], lhsT=ccodes[h][:, cols].bitcast(E5), lhsT_scale=cscales[h][:, cols],
                                rhs=rcodes[:, 128:640].bitcast(E4), rhs_scale=rscales[:, 128:640], start=True, stop=True)
            ob[(h, t)] = bk

        def o0f(h, t):
            nc.vector.scalar_tensor_tensor(out=o0[h][:, t, :], in0=xneg[:, h, t, :], scalar=rsum[h][:, t:t + 1],
                                           in1=ob[(h, t)][:, 0:128], op0=ALU.mult, op1=ALU.add)

        def col():
            nc.vector.tensor_tensor(out=colsum[:], in0=acc[:, 0:4], in1=acc[:, 4:8], op=ALU.add)

        def o1m(s, h, b):
            if h == 0:
                ob[s] = bank(b)
            cols = slice(128 * s, 128 * s + 128)
            nc.tensor.matmul_mx(out=ob[s][:], lhsT=tcodes[h][:, cols].bitcast(E5), lhsT_scale=tscales[h][:, cols],
                                rhs=rcodes[:, 256 * h:256 * h + 512].bitcast(E4),
                                rhs_scale=rscales[:, 256 * h:256 * h + 512], start=(h == 0), stop=(h == 1))

        def o1f(s):
            nc.vector.scalar_tensor_tensor(out=o1[:, s, :], in0=cneg[:, s, :], scalar=colsum[:, s:s + 1],
                                           in1=ob[s][:, 0:128], op0=ALU.mult, op1=ALU.add)

        def st0(h, t0, nt):
            nc.sync.dma_start(out=out_0[512 * h:512 * h + 512, :].rearrange("(p t) k -> p t k", t=4)[:, t0:t0 + nt, :],
                              in_=o0[h][:, t0:t0 + nt, :])

        def st1(s0, ns):
            nc.sync.dma_start(out=out_1.rearrange("(m s) k -> m s k", s=4)[:, s0:s0 + ns, :], in_=o1[:, s0:s0 + ns, :])

        load_w(3)
        load_s()
        load_w(1)
        load_d(0)
        load_u(2)
        load_w(0)
        load_u(0)
        load_u(1)
        load_u(3)
        load_u(4)
        load_w(2)
        load_x()
        load_d(1)
        load_u(5)
        load_c()
        load_u(6)
        wc(3, 0, "s")
        sigma()
        wc(1, 0, "s")
        wc(1, 1, "v")
        wc(3, 1, "s")
        wq(1)
        dt(0, 1, 0)
        wq(3)
        dt(0, 2, 1)
        dx(0, 1)
        dt(0, 3, 2)
        dt(0, 0, 3)
        dx(0, 2)
        dm(0, 1)
        dx(0, 3)
        dm(0, 2)
        dx(0, 0)
        dm(0, 3)
        m(2)
        wc(0, 0, "s")
        ut(2, 1, 4)
        wc(0, 1, "v")
        load_u(7)
        ut(2, 0, 5)
        m(0)
        ut(0, 0, 6)
        wq(0)
        load_u(8)
        m(1)
        uc(0, 0, "s")
        uc(2, 0, "s")
        ut(1, 0, 7)
        dm(0, 0)
        load_u(10)
        load_u(9)
        uc(2, 1, "v")
        uc(1, 0, "s")
        uq(0, 0)
        uq(0, 1)
        mx(0, 0, 0, 0)
        m(3)
        mx(0, 0, 2, 1)
        mx(0, 1, 0)
        mx(0, 0, 1, 2)
        mx(0, 1, 1)
        mx(0, 1, 2)
        ut(3, 0, 6)
        ut(3, 1, 5)
        m(4)
        uc(3, 0, "s")
        mx(0, 0, 3, 3)
        mx(0, 1, 3)
        uc(3, 1, "s")
        ut(4, 0, 4)
        wc(2, 0, "s")
        neg()
        xc(1, "v")
        wc(2, 1, "v")
        xc(0, "s")
        ut(4, 1, 7)
        rq(256, 128)
        uc(4, 0, "s")
        rq(0, 128)
        wq(2)
        uc(4, 1, "s")
        dt(1, 0, 6)
        uq(0, 2)
        dt(1, 3, 5)
        uq(0, 3)
        dx(1, 0)
        dt(1, 1, 4)
        mx(0, 2, 0)
        dx(1, 3)
        dm(1, 0)
        mx(0, 3, 0)
        dx(1, 1)
        mx(0, 2, 1)
        dm(1, 3)
        mx(0, 3, 1)
        mx(0, 2, 2)
        es(0, 0)
        mx(0, 3, 2)
        mx(0, 2, 3)
        mx(0, 3, 3)
        es(0, 1)
        cc("s")
        et(0, 0, 7)
        es(0, 2)
        et(0, 1, 6)
        rq(128, 128)
        ec(0, 0, "s")
        es(0, 3)
        et(0, 2, 5)
        ec(0, 1, "s")
        dt(1, 2, 0)
        m(5)
        il(0, 0, 1, "s")
        et(0, 3, 2)
        rm(0, 1)
        dx(1, 2)
        il(0, 1, 1, "s")
        il(0, 3, 1, "s")
        m(6)
        il(0, 2, 1, "s")
        ut(5, 0, 7)
        ut(5, 1, 3)
        rr(0, "s")
        ut(6, 0, 6)
        uc(5, 0, "s")
        ilq(0, 0, 4)
        ec(0, 2, "s")
        ut(6, 1, 1)
        m(7)
        uc(5, 1, "s")
        o0m(0, 2, 7)
        uc(6, 0, "s")
        o0m(0, 1, 5)
        o0m(0, 3, 3)
        uc(6, 1, "s")
        ut(7, 1, 6)
        ec(0, 3, "s")
        uq(1, 0)
        ut(7, 0, 1)
        o0f(0, 3)
        o0f(0, 1)
        uc(7, 1, "s")
        uq(1, 1)
        mx(1, 0, 2, 2)
        mx(1, 0, 0, 3)
        uc(7, 0, "s")
        m(8)
        mx(1, 0, 3, 5)
        mx(1, 1, 3)
        mx(1, 1, 0)
        ut(8, 0, 6)
        m(9)
        uq(1, 3, 0, 2)
        ut(9, 0, 1)
        uc(8, 0, "s")
        o0f(0, 2)
        mx(1, 1, 2)
        m(10)
        mx(1, 0, 1, 7)
        uc(9, 0, "s")
        mx(1, 1, 1)
        uq(1, 3, 2, 1)
        ut(10, 0, 6)
        uq(1, 2)
        o0m(0, 0, 1)
        dm(1, 2)
        uc(10, 0, "s")
        mx(1, 2, 1)
        mx(1, 2, 3)
        o0f(0, 0)
        uq(1, 3, 3, 1)
        mx(1, 2, 2)
        eq(0, 0, 4)
        st0(0, 0, 4)
        mx(1, 2, 0)
        mx(1, 3, 0)
        dm(1, 1)
        mx(1, 3, 1)
        o1m(0, 0, 6)
        mx(1, 3, 2)
        es(1, 0)
        mx(1, 3, 3)
        o1m(2, 0, 0)
        es(1, 1)
        o1m(1, 0, 1)
        o1m(3, 0, 4)
        es(1, 2)
        et(1, 0, 3)
        et(1, 1, 7)
        es(1, 3)
        ec(1, 0, "s")
        et(1, 2, 2)
        col()
        et(1, 3, 5)
        il(1, 1, 1, "v")
        il(1, 3, 1, "s")
        il(1, 0, 1, "v")
        rm(1, 3)
        ec(1, 2, "s")
        il(1, 2, 1, "v")
        ilq(1, 0, 2)
        ec(1, 1, "s")
        ilq(1, 2, 2)
        ec(1, 3, "v")
        rr(1, "s")
        eq(1, 1, 1)
        o0m(1, 3, 2)
        eq(1, 2, 2)
        o0m(1, 0, 7)
        eq(1, 0, 1)
        o0m(1, 2, 5)
        o0f(1, 3)
        o1m(1, 1, 1)
        o0f(1, 0)
        o0m(1, 1, 3)
        o0f(1, 2)
        o1m(0, 1, 6)
        o1f(1)
        o1m(2, 1, 0)
        st0(1, 2, 2)
        o0f(1, 1)
        o1m(3, 1, 4)
        o1f(0)
        st0(1, 0, 2)
        o1f(2)
        st1(0, 2)
        o1f(3)
        st1(2, 2)
